import numpy as np
import ml_dtypes


def mxq(x, axis, fmt="e4m3"):
    dtype, down = {"e4m3": (ml_dtypes.float8_e4m3fn, 7), "e5m2": (ml_dtypes.float8_e5m2, 14)}[fmt]
    v = np.moveaxis(np.asarray(x, np.float32).astype(ml_dtypes.bfloat16).astype(np.float64), axis, -1)
    blocks = v.reshape(v.shape[:-1] + (-1, 32))
    amax = np.abs(blocks).max(-1, keepdims=True)
    byte = np.maximum(np.where(amax > 0, np.frexp(amax)[1] - 1 + 127, 0) - down, 1)
    scale = np.exp2(byte - 127.0)
    codes = (blocks / scale).astype(np.float32).astype(dtype).astype(np.float64)
    return np.moveaxis((codes * scale).reshape(v.shape), -1, axis)


WIDE = False


def mx_kscale(k):
    if not WIDE:
        return np.ones(k)
    levels = np.array([10, -10, 5, -5, 0])
    a = np.random.permutation(np.resize(levels, k // 512 * 4)).reshape(k // 512, 4)
    idx = np.arange(k)
    return np.exp2(a[idx // 512, idx % 128 // 32])


BF16 = ml_dtypes.bfloat16


def bf(x):
    return np.asarray(x, np.float32).astype(BF16)


def f64(x):
    return np.asarray(x).astype(np.float64)


B, A, S, R, H = 8192, 32, 64, 1024, 512


def elu(v):
    return np.where(v > 0.0, v, np.exp(np.minimum(v, 0.0)) - 1.0)


def softplus(v):
    return np.maximum(v, 0.0) + np.log(1.0 + np.exp(-np.abs(v)))


def setup_inputs():
    s = mx_kscale(R)
    return {"rnn_hidden": bf(np.random.standard_normal((B, R)) * 0.7 * s),
            "eps": bf(np.random.standard_normal((B, S))),
            "W_h": bf(np.random.standard_normal((H, R)) * 1.4 / np.sqrt(R) / s[None, :]),
            "b_h": bf(np.random.standard_normal(H) * 0.3),
            "W_out": bf(np.random.standard_normal((2 * S, H)) * 1.5 / np.sqrt(H)),
            "b_out": bf(np.random.standard_normal(2 * S) * 0.3)}


def reference(rnn_hidden, eps, W_h, b_h, W_out, b_out):
    h2 = elu((mxq(f64(rnn_hidden), 1, "e4m3") @ mxq(f64(W_h), 1, "e4m3").T) + f64(b_h))
    o = (mxq(h2, 1, "e4m3") @ mxq(f64(W_out), 1, "e4m3").T) + f64(b_out)
    mean, std_pre = np.split(o, 2, axis=-1)
    std = softplus(std_pre) + 0.1
    new_sample = mean + std * f64(eps)
    return (mean, std, new_sample)

@@ -1,0 +1,214 @@
+from contextlib import ExitStack
+
+import concourse.mybir as mybir
+from concourse.masks import make_identity
+
+F32 = mybir.dt.float32
+BF16 = mybir.dt.bfloat16
+U32 = mybir.dt.uint32
+U8 = mybir.dt.uint8
+FP8X4 = mybir.dt.float8_e4m3fn_x4
+ACT = mybir.ActivationFunctionType
+ALU = mybir.AluOpType
+
+BATCH, R, H, S = 8192, 1024, 512, 64
+P = 128
+PACK = 4
+K_PASS = P * PACK
+PASSES = R // K_PASS
+BLOCKS = 4
+COLS = BLOCKS * P
+H_TILES = H // P
+J = BATCH // P
+CHUNKS = J // BLOCKS
+GROUP_CHUNKS = 4
+GROUP_J = GROUP_CHUNKS * BLOCKS
+
+FLOPS = 2 * BATCH * R * H + 2 * BATCH * H * 2 * S
+
+
+def quantise_k_last(nc, pools, ident, dram_rows, codes, scales):
+    rows = pools["rows"].tile([P, BLOCKS, R], BF16)
+    nc.sync.dma_start(out=rows[:], in_=dram_rows)
+    grouped = pools["grouped"].tile([P, PASSES, COLS * PACK], BF16, align_bytes=64)
+    for g in range(PASSES):
+        grouped_words = grouped[:, g, :].bitcast(F32).rearrange("p (c u) -> p c u", u=2)
+        for pair in range(BLOCKS // 2):
+            flipped = pools["flipped"].tile([P, 2, 2 * P], F32)
+            for u in range(2):
+                for n in range(2):
+                    first_word = (2 * g + u) * P
+                    nc.tensor.transpose(
+                        flipped[:, u, n * P : (n + 1) * P],
+                        rows[:, 2 * pair + n, :].bitcast(F32)[:, first_word : first_word + P],
+                        ident[:],
+                    )
+            columns = grouped_words[:, pair * 2 * P : (pair + 1) * 2 * P, :]
+            if pair == 0:
+                nc.vector.tensor_copy(out=columns, in_=flipped[:].rearrange("p u c -> p c u"))
+            else:
+                nc.scalar.copy(out=columns, in_=flipped[:].rearrange("p u c -> p c u"))
+    nc.vector.quantize_mx(
+        out=codes.bitcast(FP8X4), scales=scales, in_=grouped[:].rearrange("p g c -> p (g c)")
+    )
+
+
+def finish_group(nc, pools, group, mean_pre, expneg, floor, noise, outs):
+    js = slice(group * GROUP_J, (group + 1) * GROUP_J)
+    nc.sync.dma_start(out=outs[0][:, js, :], in_=mean_pre[:, 0, :, :])
+    log1p = pools["tail"].tile([P, GROUP_J, S], F32)
+    nc.scalar.activation(out=log1p[:], in_=expneg[:], func=ACT.Ln, bias=1.0, scale=1.0)
+    std = pools["tail"].tile([P, GROUP_J, S], F32)
+    nc.vector.tensor_tensor(out=std[:], in0=floor[:], in1=log1p[:], op=ALU.add)
+    nc.sync.dma_start(out=outs[1][:, js, :], in_=std[:])
+    sample = pools["tail"].tile([P, GROUP_J, S], F32)
+    nc.vector.tensor_tensor(out=sample[:], in0=std[:], in1=noise[:], op=ALU.mult)
+    nc.vector.tensor_tensor(out=sample[:], in0=sample[:], in1=mean_pre[:, 0, :, :], op=ALU.add)
+    nc.sync.dma_start(out=outs[2][:, js, :], in_=sample[:])
+
+
+def tile_prior_pb_t_kernel(
+    tc, rnn_hidden, eps, W_h, b_h, W_out, b_out, out_0, out_1, out_2
+):
+    nc = tc.nc
+    x_rows = rnn_hidden.rearrange("(p j) r -> p j r", j=J)
+    eps_rows = eps.rearrange("(p j) s -> p j s", j=J)
+    outs = [o.rearrange("(p j) s -> p j s", j=J) for o in (out_0, out_1, out_2)]
+
+    with ExitStack() as ctx:
+        const = ctx.enter_context(tc.tile_pool(name="const", bufs=1))
+        pools = {
+            "rows": ctx.enter_context(tc.tile_pool(name="rows", bufs=4)),
+            "grouped": ctx.enter_context(tc.tile_pool(name="grouped", bufs=2)),
+            "packed": ctx.enter_context(tc.tile_pool(name="packed", bufs=2)),
+            "elu": ctx.enter_context(tc.tile_pool(name="elu", bufs=2)),
+            "tail": ctx.enter_context(tc.tile_pool(name="tail", bufs=2)),
+            "flipped": ctx.enter_context(tc.psum_pool(name="flipped", bufs=2)),
+            "pre": ctx.enter_context(tc.psum_pool(name="pre", bufs=4)),
+            "head": ctx.enter_context(tc.psum_pool(name="head", bufs=2)),
+        }
+
+        ident = const.tile([P, P], F32)
+        make_identity(nc, ident[:])
+
+        wh_codes = const.tile([P, PASSES, COLS], U32, align_bytes=64)
+        wh_scales = const.tile([P, PASSES, COLS], U8, align_bytes=64)
+        quantise_k_last(
+            nc,
+            pools,
+            ident,
+            W_h.rearrange("(p t) r -> p t r", t=H_TILES),
+            wh_codes[:].rearrange("p g c -> p (g c)"),
+            wh_scales[:].rearrange("p g c -> p (g c)"),
+        )
+        bh_bf16 = const.tile([P, H_TILES], BF16)
+        nc.scalar.dma_start(out=bh_bf16[:], in_=b_h.rearrange("(p t) -> p t", t=H_TILES))
+        bh = const.tile([P, H_TILES], F32)
+        nc.vector.tensor_copy(out=bh[:], in_=bh_bf16[:])
+
+        wo_rows = const.tile([P, H], BF16)
+        nc.scalar.dma_start(out=wo_rows[:], in_=W_out)
+        wo_words = wo_rows[:].bitcast(F32).rearrange("o (p u) -> o u p", u=2)
+        wo_flipped = pools["flipped"].tile([P, 2, P], F32, tag="flipped")
+        for u in range(2):
+            nc.tensor.transpose(wo_flipped[:, u, :], wo_words[:, u, :], ident[:])
+        wo_grouped = const.tile([P, P * PACK], BF16, align_bytes=64)
+        nc.vector.tensor_copy(
+            out=wo_grouped[:].bitcast(F32).rearrange("p (o u) -> p o u", u=2),
+            in_=wo_flipped[:].rearrange("p u o -> p o u"),
+        )
+        wo_codes = const.tile([P, P], U32, align_bytes=64)
+        wo_scales = const.tile([P, P], U8, align_bytes=64)
+        nc.vector.quantize_mx(out=wo_codes[:].bitcast(FP8X4), scales=wo_scales[:], in_=wo_grouped[:])
+
+        bo = const.tile([P, 2 * S], BF16)
+        nc.scalar.dma_start(out=bo[:], in_=b_out.partition_broadcast(P))
+
+        for group in range(CHUNKS // GROUP_CHUNKS):
+            mean_pre = pools["tail"].tile([P, 2, GROUP_J, S], F32)
+            expneg = pools["tail"].tile([P, GROUP_J, S], F32)
+            floor = pools["tail"].tile([P, GROUP_J, S], F32)
+            noise = pools["tail"].tile([P, GROUP_J, S], BF16)
+            nc.sync.dma_start(out=noise[:], in_=eps_rows[:, group * GROUP_J : (group + 1) * GROUP_J, :])
+            for member in range(GROUP_CHUNKS):
+                chunk = group * GROUP_CHUNKS + member
+                x_codes = pools["packed"].tile([P, PASSES, COLS], U32, align_bytes=64)
+                x_scales = pools["packed"].tile([P, PASSES, COLS], U8, align_bytes=64)
+                quantise_k_last(
+                    nc,
+                    pools,
+                    ident,
+                    x_rows[:, chunk * BLOCKS : (chunk + 1) * BLOCKS, :],
+                    x_codes[:].rearrange("p g c -> p (g c)"),
+                    x_scales[:].rearrange("p g c -> p (g c)"),
+                )
+
+                grown = pools["elu"].tile([P, H_TILES, COLS], F32)
+                kept = pools["elu"].tile([P, H_TILES, COLS], F32)
+                for t in range(H_TILES):
+                    pre = pools["pre"].tile([P, COLS], F32)
+                    for g in range(PASSES):
+                        nc.tensor.matmul_mx(
+                            out=pre[:],
+                            lhsT=wh_codes[:, g, t * P : (t + 1) * P].bitcast(FP8X4),
+                            lhsT_scale=wh_scales[:, g, t * P : (t + 1) * P],
+                            rhs=x_codes[:, g, :].bitcast(FP8X4),
+                            rhs_scale=x_scales[:, g, :],
+                            start=(g == 0),
+                            stop=(g == PASSES - 1),
+                        )
+                    nc.scalar.activation(
+                        out=grown[:, t, :], in_=pre[:], func=ACT.Exp, bias=bh[:, t : t + 1], scale=1.0
+                    )
+                    nc.scalar.activation(
+                        out=kept[:, t, :], in_=pre[:], func=ACT.Relu, bias=bh[:, t : t + 1], scale=1.0
+                    )
+                h2 = pools["elu"].tile([P, COLS, PACK], BF16, align_bytes=64)
+                nc.vector.scalar_tensor_tensor(
+                    out=h2[:],
+                    in0=grown[:].rearrange("p t c -> p c t"),
+                    scalar=-1.0,
+                    in1=kept[:].rearrange("p t c -> p c t"),
+                    op0=ALU.add,
+                    op1=ALU.min,
+                )
+                h2_codes = pools["packed"].tile([P, COLS], U32, align_bytes=64)
+                h2_scales = pools["packed"].tile([P, COLS], U8, align_bytes=64)
+                nc.vector.quantize_mx(
+                    out=h2_codes[:].bitcast(FP8X4),
+                    scales=h2_scales[:],
+                    in_=h2[:].rearrange("p c t -> p (c t)"),
+                )
+
+                head = pools["head"].tile([P, BLOCKS, 2 * S], F32)
+                for n in range(BLOCKS):
+                    nc.tensor.matmul_mx(
+                        out=head[:, n, :],
+                        lhsT=h2_codes[:, n * P : (n + 1) * P].bitcast(FP8X4),
+                        lhsT_scale=h2_scales[:, n * P : (n + 1) * P],
+                        rhs=wo_codes[:].bitcast(FP8X4),
+                        rhs_scale=wo_scales[:],
+                        start=True,
+                        stop=True,
+                    )
+                js = slice(member * BLOCKS, (member + 1) * BLOCKS)
+                nc.vector.tensor_tensor(
+                    out=mean_pre[:, :, js, :].rearrange("p half j s -> p j half s"),
+                    in0=head[:].rearrange("p j (half s) -> p j half s", half=2),
+                    in1=bo[:]
+                    .rearrange("p (half s) -> p half s", half=2)
+                    .unsqueeze(1)
+                    .to_broadcast([P, BLOCKS, 2, S]),
+                    op=ALU.add,
+                )
+                nc.scalar.activation(out=expneg[:, js, :], in_=mean_pre[:, 1, js, :], func=ACT.Abs)
+                nc.scalar.activation(out=expneg[:, js, :], in_=expneg[:, js, :], func=ACT.Exp, scale=-1.0)
+                nc.vector.tensor_scalar(
+                    out=floor[:, js, :],
+                    in0=mean_pre[:, 1, js, :],
+                    scalar1=0.0,
+                    scalar2=0.1,
+                    op0=ALU.max,
+                    op1=ALU.add,
+                )
+            finish_group(nc, pools, group, mean_pre, expneg, floor, noise, outs)

@@ -27,46 +27,6 @@ GROUP_J = GROUP_CHUNKS * BLOCKS
 FLOPS = 2 * BATCH * R * H + 2 * BATCH * H * 2 * S
 
 
-def quantise_k_last(nc, pools, ident, dram_rows, codes, scales):
-    rows = pools["rows"].tile([P, BLOCKS, R], BF16)
-    nc.sync.dma_start(out=rows[:], in_=dram_rows)
-    grouped = pools["grouped"].tile([P, PASSES, COLS * PACK], BF16, align_bytes=64)
-    for g in range(PASSES):
-        grouped_words = grouped[:, g, :].bitcast(F32).rearrange("p (c u) -> p c u", u=2)
-        for pair in range(BLOCKS // 2):
-            flipped = pools["flipped"].tile([P, 2, 2 * P], F32)
-            for u in range(2):
-                for n in range(2):
-                    first_word = (2 * g + u) * P
-                    nc.tensor.transpose(
-                        flipped[:, u, n * P : (n + 1) * P],
-                        rows[:, 2 * pair + n, :].bitcast(F32)[:, first_word : first_word + P],
-                        ident[:],
-                    )
-            columns = grouped_words[:, pair * 2 * P : (pair + 1) * 2 * P, :]
-            if pair == 0:
-                nc.vector.tensor_copy(out=columns, in_=flipped[:].rearrange("p u c -> p c u"))
-            else:
-                nc.scalar.copy(out=columns, in_=flipped[:].rearrange("p u c -> p c u"))
-    nc.vector.quantize_mx(
-        out=codes.bitcast(FP8X4), scales=scales, in_=grouped[:].rearrange("p g c -> p (g c)")
-    )
-
-
-def finish_group(nc, pools, group, mean_pre, expneg, floor, noise, outs):
-    js = slice(group * GROUP_J, (group + 1) * GROUP_J)
-    nc.sync.dma_start(out=outs[0][:, js, :], in_=mean_pre[:, 0, :, :])
-    log1p = pools["tail"].tile([P, GROUP_J, S], F32)
-    nc.scalar.activation(out=log1p[:], in_=expneg[:], func=ACT.Ln, bias=1.0, scale=1.0)
-    std = pools["tail"].tile([P, GROUP_J, S], F32)
-    nc.vector.tensor_tensor(out=std[:], in0=floor[:], in1=log1p[:], op=ALU.add)
-    nc.sync.dma_start(out=outs[1][:, js, :], in_=std[:])
-    sample = pools["tail"].tile([P, GROUP_J, S], F32)
-    nc.vector.tensor_tensor(out=sample[:], in0=std[:], in1=noise[:], op=ALU.mult)
-    nc.vector.tensor_tensor(out=sample[:], in0=sample[:], in1=mean_pre[:, 0, :, :], op=ALU.add)
-    nc.sync.dma_start(out=outs[2][:, js, :], in_=sample[:])
-
-
 def tile_prior_pb_t_kernel(
     tc, rnn_hidden, eps, W_h, b_h, W_out, b_out, out_0, out_1, out_2
 ):
@@ -76,40 +36,73 @@ def tile_prior_pb_t_kernel(
     outs = [o.rearrange("(p j) s -> p j s", j=J) for o in (out_0, out_1, out_2)]
 
     with ExitStack() as ctx:
+        ctx.enter_context(tc.manual_schedule())
         const = ctx.enter_context(tc.tile_pool(name="const", bufs=1))
-        pools = {
-            "rows": ctx.enter_context(tc.tile_pool(name="rows", bufs=4)),
-            "grouped": ctx.enter_context(tc.tile_pool(name="grouped", bufs=2)),
-            "packed": ctx.enter_context(tc.tile_pool(name="packed", bufs=2)),
-            "elu": ctx.enter_context(tc.tile_pool(name="elu", bufs=2)),
-            "tail": ctx.enter_context(tc.tile_pool(name="tail", bufs=2)),
-            "flipped": ctx.enter_context(tc.psum_pool(name="flipped", bufs=2)),
-            "pre": ctx.enter_context(tc.psum_pool(name="pre", bufs=4)),
-            "head": ctx.enter_context(tc.psum_pool(name="head", bufs=2)),
-        }
+        rows_pool = ctx.enter_context(tc.tile_pool(name="rows", bufs=4))
+        work = ctx.enter_context(tc.tile_pool(name="work", bufs=2))
+        tail = ctx.enter_context(tc.tile_pool(name="tail", bufs=2))
+        flipped_pool = ctx.enter_context(tc.psum_pool(name="flipped", bufs=2))
+        pre_pool = ctx.enter_context(tc.psum_pool(name="pre", bufs=H_TILES))
+        head_pool = ctx.enter_context(tc.psum_pool(name="head", bufs=2))
 
         ident = const.tile([P, P], F32)
         make_identity(nc, ident[:])
 
-        wh_codes = const.tile([P, PASSES, COLS], U32, align_bytes=64)
-        wh_scales = const.tile([P, PASSES, COLS], U8, align_bytes=64)
-        quantise_k_last(
-            nc,
-            pools,
-            ident,
-            W_h.rearrange("(p t) r -> p t r", t=H_TILES),
-            wh_codes[:].rearrange("p g c -> p (g c)"),
-            wh_scales[:].rearrange("p g c -> p (g c)"),
-        )
+        def load_rows(dram_rows):
+            rows = rows_pool.tile([P, BLOCKS, R], BF16)
+            nc.sync.dma_start(out=rows[:], in_=dram_rows)
+            return rows
+
+        def flip(rows, g):
+            banks = []
+            for pair in range(BLOCKS // 2):
+                flipped = flipped_pool.tile([P, 2, 2 * P], F32)
+                for u in range(2):
+                    for n in range(2):
+                        first_word = (2 * g + u) * P
+                        nc.tensor.transpose(
+                            flipped[:, u, n * P : (n + 1) * P],
+                            rows[:, 2 * pair + n, :].bitcast(F32)[:, first_word : first_word + P],
+                            ident[:],
+                        )
+                banks.append(flipped)
+            return banks
+
+        def regroup(banks, grouped, g):
+            words = grouped[:, g, :].bitcast(F32).rearrange("p (c u) -> p c u", u=2)
+            nc.vector.tensor_copy(
+                out=words[:, 0 : 2 * P, :], in_=banks[0][:].rearrange("p u c -> p c u")
+            )
+            nc.scalar.copy(
+                out=words[:, 2 * P : 4 * P, :], in_=banks[1][:].rearrange("p u c -> p c u")
+            )
+
+        def pack(grouped, codes, scales):
+            nc.vector.quantize_mx(
+                out=codes[:].rearrange("p g c -> p (g c)").bitcast(FP8X4),
+                scales=scales[:].rearrange("p g c -> p (g c)"),
+                in_=grouped[:].rearrange("p g c -> p (g c)"),
+            )
+
+        wh_rows = load_rows(W_h.rearrange("(p t) r -> p t r", t=H_TILES))
         bh_bf16 = const.tile([P, H_TILES], BF16)
         nc.scalar.dma_start(out=bh_bf16[:], in_=b_h.rearrange("(p t) -> p t", t=H_TILES))
+        wo_rows = const.tile([P, H], BF16)
+        nc.scalar.dma_start(out=wo_rows[:], in_=W_out)
+        bo = const.tile([P, 2 * S], BF16)
+        nc.scalar.dma_start(out=bo[:], in_=b_out.partition_broadcast(P))
+
+        wh_grouped = work.tile([P, PASSES, COLS * PACK], BF16, align_bytes=64, tag="grouped")
+        wh_codes = const.tile([P, PASSES, COLS], U32, align_bytes=64)
+        wh_scales = const.tile([P, PASSES, COLS], U8, align_bytes=64)
+        for g in range(PASSES):
+            regroup(flip(wh_rows, g), wh_grouped, g)
+        pack(wh_grouped, wh_codes, wh_scales)
         bh = const.tile([P, H_TILES], F32)
         nc.vector.tensor_copy(out=bh[:], in_=bh_bf16[:])
 
-        wo_rows = const.tile([P, H], BF16)
-        nc.scalar.dma_start(out=wo_rows[:], in_=W_out)
         wo_words = wo_rows[:].bitcast(F32).rearrange("o (p u) -> o u p", u=2)
-        wo_flipped = pools["flipped"].tile([P, 2, P], F32, tag="flipped")
+        wo_flipped = flipped_pool.tile([P, 2, P], F32, tag="flipped")
         for u in range(2):
             nc.tensor.transpose(wo_flipped[:, u, :], wo_words[:, u, :], ident[:])
         wo_grouped = const.tile([P, P * PACK], BF16, align_bytes=64)
@@ -121,94 +114,159 @@ def tile_prior_pb_t_kernel(
         wo_scales = const.tile([P, P], U8, align_bytes=64)
         nc.vector.quantize_mx(out=wo_codes[:].bitcast(FP8X4), scales=wo_scales[:], in_=wo_grouped[:])
 
-        bo = const.tile([P, 2 * S], BF16)
-        nc.scalar.dma_start(out=bo[:], in_=b_out.partition_broadcast(P))
+        rows_of, banks_of, grouped_of, packed_of = {}, {}, {}, {}
+        pre_of, halves_of, h2_of, head_of, group_of = {}, {}, {}, {}, {}
 
-        for group in range(CHUNKS // GROUP_CHUNKS):
-            mean_pre = pools["tail"].tile([P, 2, GROUP_J, S], F32)
-            expneg = pools["tail"].tile([P, GROUP_J, S], F32)
-            floor = pools["tail"].tile([P, GROUP_J, S], F32)
-            noise = pools["tail"].tile([P, GROUP_J, S], BF16)
-            nc.sync.dma_start(out=noise[:], in_=eps_rows[:, group * GROUP_J : (group + 1) * GROUP_J, :])
-            for member in range(GROUP_CHUNKS):
-                chunk = group * GROUP_CHUNKS + member
-                x_codes = pools["packed"].tile([P, PASSES, COLS], U32, align_bytes=64)
-                x_scales = pools["packed"].tile([P, PASSES, COLS], U8, align_bytes=64)
-                quantise_k_last(
-                    nc,
-                    pools,
-                    ident,
-                    x_rows[:, chunk * BLOCKS : (chunk + 1) * BLOCKS, :],
-                    x_codes[:].rearrange("p g c -> p (g c)"),
-                    x_scales[:].rearrange("p g c -> p (g c)"),
-                )
-
-                grown = pools["elu"].tile([P, H_TILES, COLS], F32)
-                kept = pools["elu"].tile([P, H_TILES, COLS], F32)
-                for t in range(H_TILES):
-                    pre = pools["pre"].tile([P, COLS], F32)
-                    for g in range(PASSES):
-                        nc.tensor.matmul_mx(
-                            out=pre[:],
-                            lhsT=wh_codes[:, g, t * P : (t + 1) * P].bitcast(FP8X4),
-                            lhsT_scale=wh_scales[:, g, t * P : (t + 1) * P],
-                            rhs=x_codes[:, g, :].bitcast(FP8X4),
-                            rhs_scale=x_scales[:, g, :],
-                            start=(g == 0),
-                            stop=(g == PASSES - 1),
-                        )
-                    nc.scalar.activation(
-                        out=grown[:, t, :], in_=pre[:], func=ACT.Exp, bias=bh[:, t : t + 1], scale=1.0
-                    )
-                    nc.scalar.activation(
-                        out=kept[:, t, :], in_=pre[:], func=ACT.Relu, bias=bh[:, t : t + 1], scale=1.0
-                    )
-                h2 = pools["elu"].tile([P, COLS, PACK], BF16, align_bytes=64)
-                nc.vector.scalar_tensor_tensor(
-                    out=h2[:],
-                    in0=grown[:].rearrange("p t c -> p c t"),
-                    scalar=-1.0,
-                    in1=kept[:].rearrange("p t c -> p c t"),
-                    op0=ALU.add,
-                    op1=ALU.min,
-                )
-                h2_codes = pools["packed"].tile([P, COLS], U32, align_bytes=64)
-                h2_scales = pools["packed"].tile([P, COLS], U8, align_bytes=64)
-                nc.vector.quantize_mx(
-                    out=h2_codes[:].bitcast(FP8X4),
-                    scales=h2_scales[:],
-                    in_=h2[:].rearrange("p c t -> p (c t)"),
-                )
-
-                head = pools["head"].tile([P, BLOCKS, 2 * S], F32)
-                for n in range(BLOCKS):
+        def first_matmul(c):
+            x_codes, x_scales = packed_of[c]
+            pre_of[c] = []
+            for t in range(H_TILES):
+                pre = pre_pool.tile([P, COLS], F32)
+                for g in range(PASSES):
                     nc.tensor.matmul_mx(
-                        out=head[:, n, :],
-                        lhsT=h2_codes[:, n * P : (n + 1) * P].bitcast(FP8X4),
-                        lhsT_scale=h2_scales[:, n * P : (n + 1) * P],
-                        rhs=wo_codes[:].bitcast(FP8X4),
-                        rhs_scale=wo_scales[:],
-                        start=True,
-                        stop=True,
+                        out=pre[:],
+                        lhsT=wh_codes[:, g, t * P : (t + 1) * P].bitcast(FP8X4),
+                        lhsT_scale=wh_scales[:, g, t * P : (t + 1) * P],
+                        rhs=x_codes[:, g, :].bitcast(FP8X4),
+                        rhs_scale=x_scales[:, g, :],
+                        start=(g == 0),
+                        stop=(g == PASSES - 1),
                     )
-                js = slice(member * BLOCKS, (member + 1) * BLOCKS)
-                nc.vector.tensor_tensor(
-                    out=mean_pre[:, :, js, :].rearrange("p half j s -> p j half s"),
-                    in0=head[:].rearrange("p j (half s) -> p j half s", half=2),
-                    in1=bo[:]
-                    .rearrange("p (half s) -> p half s", half=2)
-                    .unsqueeze(1)
-                    .to_broadcast([P, BLOCKS, 2, S]),
-                    op=ALU.add,
+                pre_of[c].append(pre)
+
+        def elu_halves(c, t):
+            grown, kept = halves_of[c]
+            pre = pre_of[c][t]
+            nc.scalar.activation(
+                out=grown[:, t, :], in_=pre[:], func=ACT.Exp, bias=bh[:, t : t + 1], scale=1.0
+            )
+            nc.scalar.activation(
+                out=kept[:, t, :], in_=pre[:], func=ACT.Relu, bias=bh[:, t : t + 1], scale=1.0
+            )
+
+        def finish_elu(c):
+            grown, kept = halves_of[c]
+            h2 = work.tile([P, COLS, PACK], BF16, align_bytes=64)
+            nc.vector.scalar_tensor_tensor(
+                out=h2[:],
+                in0=grown[:].rearrange("p t c -> p c t"),
+                scalar=-1.0,
+                in1=kept[:].rearrange("p t c -> p c t"),
+                op0=ALU.add,
+                op1=ALU.min,
+            )
+            h2_codes = work.tile([P, COLS], U32, align_bytes=64)
+            h2_scales = work.tile([P, COLS], U8, align_bytes=64)
+            nc.vector.quantize_mx(
+                out=h2_codes[:].bitcast(FP8X4),
+                scales=h2_scales[:],
+                in_=h2[:].rearrange("p c t -> p (c t)"),
+            )
+            h2_of[c] = (h2_codes, h2_scales)
+
+        def second_matmul(c):
+            h2_codes, h2_scales = h2_of[c]
+            head = head_pool.tile([P, BLOCKS, 2 * S], F32)
+            for n in range(BLOCKS):
+                nc.tensor.matmul_mx(
+                    out=head[:, n, :],
+                    lhsT=h2_codes[:, n * P : (n + 1) * P].bitcast(FP8X4),
+                    lhsT_scale=h2_scales[:, n * P : (n + 1) * P],
+                    rhs=wo_codes[:].bitcast(FP8X4),
+                    rhs_scale=wo_scales[:],
+                    start=True,
+                    stop=True,
                 )
-                nc.scalar.activation(out=expneg[:, js, :], in_=mean_pre[:, 1, js, :], func=ACT.Abs)
-                nc.scalar.activation(out=expneg[:, js, :], in_=expneg[:, js, :], func=ACT.Exp, scale=-1.0)
-                nc.vector.tensor_scalar(
-                    out=floor[:, js, :],
-                    in0=mean_pre[:, 1, js, :],
-                    scalar1=0.0,
-                    scalar2=0.1,
-                    op0=ALU.max,
-                    op1=ALU.add,
-                )
-            finish_group(nc, pools, group, mean_pre, expneg, floor, noise, outs)
+            head_of[c] = head
+
+        def open_group(group):
+            mean_pre = tail.tile([P, 2, GROUP_J, S], F32)
+            expneg = tail.tile([P, GROUP_J, S], F32)
+            floor = tail.tile([P, GROUP_J, S], F32)
+            noise = tail.tile([P, GROUP_J, S], BF16)
+            nc.sync.dma_start(out=noise[:], in_=eps_rows[:, group * GROUP_J : (group + 1) * GROUP_J, :])
+            group_of[group] = (mean_pre, expneg, floor, noise)
+
+        def add_bias(c):
+            mean_pre, expneg, floor, noise = group_of[c // GROUP_CHUNKS]
+            js = slice((c % GROUP_CHUNKS) * BLOCKS, (c % GROUP_CHUNKS + 1) * BLOCKS)
+            nc.vector.tensor_tensor(
+                out=mean_pre[:, :, js, :].rearrange("p half j s -> p j half s"),
+                in0=head_of[c][:].rearrange("p j (half s) -> p j half s", half=2),
+                in1=bo[:]
+                .rearrange("p (half s) -> p half s", half=2)
+                .unsqueeze(1)
+                .to_broadcast([P, BLOCKS, 2, S]),
+                op=ALU.add,
+            )
+            nc.vector.tensor_scalar(
+                out=floor[:, js, :],
+                in0=mean_pre[:, 1, js, :],
+                scalar1=0.0,
+                scalar2=0.1,
+                op0=ALU.max,
+                op1=ALU.add,
+            )
+            nc.scalar.activation(out=expneg[:, js, :], in_=mean_pre[:, 1, js, :], func=ACT.Abs)
+            nc.scalar.activation(out=expneg[:, js, :], in_=expneg[:, js, :], func=ACT.Exp, scale=-1.0)
+
+        def take_logs(group):
+            mean_pre, expneg, floor, noise = group_of[group]
+            nc.scalar.activation(out=expneg[:], in_=expneg[:], func=ACT.Ln, bias=1.0, scale=1.0)
+
+        def finish_group(group):
+            mean_pre, log1p, floor, noise = group_of[group]
+            js = slice(group * GROUP_J, (group + 1) * GROUP_J)
+            nc.sync.dma_start(out=outs[0][:, js, :], in_=mean_pre[:, 0, :, :])
+            std = tail.tile([P, GROUP_J, S], F32)
+            nc.vector.tensor_tensor(out=std[:], in0=floor[:], in1=log1p[:], op=ALU.add)
+            nc.sync.dma_start(out=outs[1][:, js, :], in_=std[:])
+            sample = tail.tile([P, GROUP_J, S], F32)
+            nc.vector.tensor_tensor(out=sample[:], in0=std[:], in1=noise[:], op=ALU.mult)
+            nc.vector.tensor_tensor(out=sample[:], in0=sample[:], in1=mean_pre[:, 0, :, :], op=ALU.add)
+            nc.sync.dma_start(out=outs[2][:, js, :], in_=sample[:])
+
+        def live(c):
+            return 0 <= c < CHUNKS
+
+        def closes_group(c):
+            return live(c) and c % GROUP_CHUNKS == GROUP_CHUNKS - 1
+
+        for i in range(-3, CHUNKS + 2):
+            if live(i + 3):
+                rows_of[i + 3] = load_rows(x_rows[:, (i + 3) * BLOCKS : (i + 4) * BLOCKS, :])
+            if live(i + 1):
+                regroup(banks_of[i + 1], grouped_of[i + 1], 0)
+                banks_of[i + 1] = flip(rows_of[i + 1], 1)
+            if live(i - 1):
+                finish_elu(i - 1)
+                second_matmul(i - 1)
+            if closes_group(i - 2):
+                finish_group((i - 2) // GROUP_CHUNKS)
+            if live(i):
+                grown = work.tile([P, H_TILES, COLS], F32)
+                kept = work.tile([P, H_TILES, COLS], F32)
+                halves_of[i] = (grown, kept)
+                elu_halves(i, 0)
+                elu_halves(i, 1)
+            if live(i + 1):
+                regroup(banks_of[i + 1], grouped_of[i + 1], 1)
+                x_codes = work.tile([P, PASSES, COLS], U32, align_bytes=64)
+                x_scales = work.tile([P, PASSES, COLS], U8, align_bytes=64)
+                packed_of[i + 1] = (x_codes, x_scales)
+                pack(grouped_of[i + 1], x_codes, x_scales)
+            if live(i + 2):
+                grouped = work.tile([P, PASSES, COLS * PACK], BF16, align_bytes=64)
+                grouped_of[i + 2] = grouped
+                banks_of[i + 2] = flip(rows_of[i + 2], 0)
+            if live(i):
+                elu_halves(i, 2)
+                elu_halves(i, 3)
+            if live(i + 1):
+                first_matmul(i + 1)
+            if live(i - 1):
+                if (i - 1) % GROUP_CHUNKS == 0:
+                    open_group((i - 1) // GROUP_CHUNKS)
+                add_bias(i - 1)
+            if closes_group(i - 1):
+                take_logs((i - 1) // GROUP_CHUNKS)

@@ -70,12 +70,11 @@ def tile_prior_pb_t_kernel(
 
         def regroup(banks, grouped, g):
             words = grouped[:, g, :].bitcast(F32).rearrange("p (c u) -> p c u", u=2)
-            nc.vector.tensor_copy(
-                out=words[:, 0 : 2 * P, :], in_=banks[0][:].rearrange("p u c -> p c u")
-            )
-            nc.scalar.copy(
-                out=words[:, 2 * P : 4 * P, :], in_=banks[1][:].rearrange("p u c -> p c u")
-            )
+            for pair in range(BLOCKS // 2):
+                nc.scalar.copy(
+                    out=words[:, pair * 2 * P : (pair + 1) * 2 * P, :],
+                    in_=banks[pair][:].rearrange("p u c -> p c u"),
+                )
 
         def pack(grouped, codes, scales):
             nc.vector.quantize_mx(
@@ -115,7 +114,8 @@ def tile_prior_pb_t_kernel(
         nc.vector.quantize_mx(out=wo_codes[:].bitcast(FP8X4), scales=wo_scales[:], in_=wo_grouped[:])
 
         rows_of, banks_of, grouped_of, packed_of = {}, {}, {}, {}
-        pre_of, halves_of, h2_of, head_of, group_of = {}, {}, {}, {}, {}
+        pre_of, grown_of, planes_of, h2_of, head_of, group_of = {}, {}, {}, {}, {}, {}
+        log1p_of = {}
 
         def first_matmul(c):
             x_codes, x_scales = packed_of[c]
@@ -134,26 +134,36 @@ def tile_prior_pb_t_kernel(
                     )
                 pre_of[c].append(pre)
 
-        def elu_halves(c, t):
-            grown, kept = halves_of[c]
-            pre = pre_of[c][t]
-            nc.scalar.activation(
-                out=grown[:, t, :], in_=pre[:], func=ACT.Exp, bias=bh[:, t : t + 1], scale=1.0
-            )
-            nc.scalar.activation(
-                out=kept[:, t, :], in_=pre[:], func=ACT.Relu, bias=bh[:, t : t + 1], scale=1.0
-            )
+        def grow(c):
+            grown = work.tile([P, H_TILES, COLS], F32)
+            for t in range(H_TILES):
+                nc.scalar.activation(
+                    out=grown[:, t, :], in_=pre_of[c][t][:], func=ACT.Exp, bias=bh[:, t : t + 1], scale=1.0
+                )
+            grown_of[c] = grown
 
         def finish_elu(c):
-            grown, kept = halves_of[c]
+            below = work.tile([P, H_TILES, COLS], F32)
+            nc.vector.tensor_scalar(
+                out=below[:], in0=grown_of[c][:], scalar1=-1.0, scalar2=0.0, op0=ALU.add, op1=ALU.min
+            )
+            h2_planes = work.tile([P, H_TILES, COLS], BF16)
+            for t in range(H_TILES):
+                nc.vector.scalar_tensor_tensor(
+                    out=h2_planes[:, t, :],
+                    in0=pre_of[c][t][:],
+                    scalar=bh[:, t : t + 1],
+                    in1=below[:, t, :],
+                    op0=ALU.add,
+                    op1=ALU.max,
+                )
+            planes_of[c] = h2_planes
+
+        def pack_h2(c):
             h2 = work.tile([P, COLS, PACK], BF16, align_bytes=64)
-            nc.vector.scalar_tensor_tensor(
-                out=h2[:],
-                in0=grown[:].rearrange("p t c -> p c t"),
-                scalar=-1.0,
-                in1=kept[:].rearrange("p t c -> p c t"),
-                op0=ALU.add,
-                op1=ALU.min,
+            nc.vector.tensor_copy(
+                out=h2[:].rearrange("p (c i) t -> p c t i", i=4),
+                in_=planes_of[c][:].rearrange("p t (c i) -> p c t i", i=4),
             )
             h2_codes = work.tile([P, COLS], U32, align_bytes=64)
             h2_scales = work.tile([P, COLS], U8, align_bytes=64)
@@ -199,27 +209,33 @@ def tile_prior_pb_t_kernel(
                 .to_broadcast([P, BLOCKS, 2, S]),
                 op=ALU.add,
             )
-            nc.vector.tensor_scalar(
-                out=floor[:, js, :],
-                in0=mean_pre[:, 1, js, :],
-                scalar1=0.0,
-                scalar2=0.1,
-                op0=ALU.max,
-                op1=ALU.add,
-            )
+
+        def soften(c):
+            mean_pre, expneg, floor, noise = group_of[c // GROUP_CHUNKS]
+            js = slice((c % GROUP_CHUNKS) * BLOCKS, (c % GROUP_CHUNKS + 1) * BLOCKS)
+            nc.scalar.activation(out=floor[:, js, :], in_=mean_pre[:, 1, js, :], func=ACT.Relu)
             nc.scalar.activation(out=expneg[:, js, :], in_=mean_pre[:, 1, js, :], func=ACT.Abs)
             nc.scalar.activation(out=expneg[:, js, :], in_=expneg[:, js, :], func=ACT.Exp, scale=-1.0)
 
         def take_logs(group):
             mean_pre, expneg, floor, noise = group_of[group]
-            nc.scalar.activation(out=expneg[:], in_=expneg[:], func=ACT.Ln, bias=1.0, scale=1.0)
+            log1p = tail.tile([P, GROUP_J, S], F32)
+            nc.scalar.activation(out=log1p[:], in_=expneg[:], func=ACT.Ln, bias=1.0, scale=1.0)
+            log1p_of[group] = log1p
 
         def finish_group(group):
-            mean_pre, log1p, floor, noise = group_of[group]
+            mean_pre, expneg, floor, noise = group_of[group]
             js = slice(group * GROUP_J, (group + 1) * GROUP_J)
             nc.sync.dma_start(out=outs[0][:, js, :], in_=mean_pre[:, 0, :, :])
             std = tail.tile([P, GROUP_J, S], F32)
-            nc.vector.tensor_tensor(out=std[:], in0=floor[:], in1=log1p[:], op=ALU.add)
+            nc.vector.scalar_tensor_tensor(
+                out=std[:].rearrange("p j s -> p (j s)"),
+                in0=floor[:].rearrange("p j s -> p (j s)"),
+                scalar=0.1,
+                in1=log1p_of[group][:].rearrange("p j s -> p (j s)"),
+                op0=ALU.add,
+                op1=ALU.add,
+            )
             nc.sync.dma_start(out=outs[1][:, js, :], in_=std[:])
             sample = tail.tile([P, GROUP_J, S], F32)
             nc.vector.tensor_tensor(out=sample[:], in0=std[:], in1=noise[:], op=ALU.mult)
@@ -232,41 +248,38 @@ def tile_prior_pb_t_kernel(
         def closes_group(c):
             return live(c) and c % GROUP_CHUNKS == GROUP_CHUNKS - 1
 
-        for i in range(-3, CHUNKS + 2):
-            if live(i + 3):
-                rows_of[i + 3] = load_rows(x_rows[:, (i + 3) * BLOCKS : (i + 4) * BLOCKS, :])
-            if live(i + 1):
-                regroup(banks_of[i + 1], grouped_of[i + 1], 0)
-                banks_of[i + 1] = flip(rows_of[i + 1], 1)
+        for i in range(-4, CHUNKS + 3):
+            if live(i + 4):
+                rows_of[i + 4] = load_rows(x_rows[:, (i + 4) * BLOCKS : (i + 5) * BLOCKS, :])
+            if live(i - 2):
+                if (i - 2) % GROUP_CHUNKS == 0:
+                    open_group((i - 2) // GROUP_CHUNKS)
+                add_bias(i - 2)
             if live(i - 1):
-                finish_elu(i - 1)
+                pack_h2(i - 1)
                 second_matmul(i - 1)
-            if closes_group(i - 2):
-                finish_group((i - 2) // GROUP_CHUNKS)
             if live(i):
-                grown = work.tile([P, H_TILES, COLS], F32)
-                kept = work.tile([P, H_TILES, COLS], F32)
-                halves_of[i] = (grown, kept)
-                elu_halves(i, 0)
-                elu_halves(i, 1)
-            if live(i + 1):
-                regroup(banks_of[i + 1], grouped_of[i + 1], 1)
-                x_codes = work.tile([P, PASSES, COLS], U32, align_bytes=64)
-                x_scales = work.tile([P, PASSES, COLS], U8, align_bytes=64)
-                packed_of[i + 1] = (x_codes, x_scales)
-                pack(grouped_of[i + 1], x_codes, x_scales)
+                grow(i)
             if live(i + 2):
                 grouped = work.tile([P, PASSES, COLS * PACK], BF16, align_bytes=64)
                 grouped_of[i + 2] = grouped
-                banks_of[i + 2] = flip(rows_of[i + 2], 0)
+                regroup(banks_of[i + 2], grouped, 0)
+                banks_of[i + 2] = flip(rows_of[i + 2], 1)
+            if live(i - 2):
+                soften(i - 2)
+            if closes_group(i - 2):
+                take_logs((i - 2) // GROUP_CHUNKS)
             if live(i):
-                elu_halves(i, 2)
-                elu_halves(i, 3)
+                finish_elu(i)
             if live(i + 1):
                 first_matmul(i + 1)
-            if live(i - 1):
-                if (i - 1) % GROUP_CHUNKS == 0:
-                    open_group((i - 1) // GROUP_CHUNKS)
-                add_bias(i - 1)
-            if closes_group(i - 1):
-                take_logs((i - 1) // GROUP_CHUNKS)
+            if closes_group(i - 3):
+                finish_group((i - 3) // GROUP_CHUNKS)
+            if live(i + 2):
+                regroup(banks_of[i + 2], grouped_of[i + 2], 1)
+                x_codes = work.tile([P, PASSES, COLS], U32, align_bytes=64)
+                x_scales = work.tile([P, PASSES, COLS], U8, align_bytes=64)
+                packed_of[i + 2] = (x_codes, x_scales)
+                pack(grouped_of[i + 2], x_codes, x_scales)
+            if live(i + 3):
+                banks_of[i + 3] = flip(rows_of[i + 3], 0)

@@ -23,6 +23,10 @@ J = BATCH // P
 CHUNKS = J // BLOCKS
 GROUP_CHUNKS = 4
 GROUP_J = GROUP_CHUNKS * BLOCKS
+V_BANKS = 3
+STD_MIN = 0.1
+EXP_MINUS_STD_MIN = 0.9048374180359595
+CAP = 30.0
 
 FLOPS = 2 * BATCH * R * H + 2 * BATCH * H * 2 * S
 
@@ -39,42 +43,45 @@ def tile_prior_pb_t_kernel(
         ctx.enter_context(tc.manual_schedule())
         const = ctx.enter_context(tc.tile_pool(name="const", bufs=1))
         rows_pool = ctx.enter_context(tc.tile_pool(name="rows", bufs=4))
+        ahead = ctx.enter_context(tc.tile_pool(name="ahead", bufs=3))
         work = ctx.enter_context(tc.tile_pool(name="work", bufs=2))
         tail = ctx.enter_context(tc.tile_pool(name="tail", bufs=2))
-        flipped_pool = ctx.enter_context(tc.psum_pool(name="flipped", bufs=2))
-        pre_pool = ctx.enter_context(tc.psum_pool(name="pre", bufs=H_TILES))
-        head_pool = ctx.enter_context(tc.psum_pool(name="head", bufs=2))
+        flipped_pool = ctx.enter_context(tc.psum_pool(name="flipped", bufs=PASSES * BLOCKS // 2))
+        pre_pool = ctx.enter_context(tc.psum_pool(name="pre", bufs=V_BANKS))
+        head_pool = ctx.enter_context(tc.psum_pool(name="head", bufs=1))
 
         ident = const.tile([P, P], F32)
         make_identity(nc, ident[:])
 
-        def load_rows(dram_rows):
-            rows = rows_pool.tile([P, BLOCKS, R], BF16)
-            nc.sync.dma_start(out=rows[:], in_=dram_rows)
-            return rows
+        def load_rows(rows, dram_rows):
+            for g in range(PASSES):
+                ks = slice(g * K_PASS, (g + 1) * K_PASS)
+                nc.sync.dma_start(out=rows[:, :, ks], in_=dram_rows[:, :, ks])
 
-        def flip(rows, g):
+        def flip(rows):
             banks = []
-            for pair in range(BLOCKS // 2):
-                flipped = flipped_pool.tile([P, 2, 2 * P], F32)
-                for u in range(2):
-                    for n in range(2):
-                        first_word = (2 * g + u) * P
-                        nc.tensor.transpose(
-                            flipped[:, u, n * P : (n + 1) * P],
-                            rows[:, 2 * pair + n, :].bitcast(F32)[:, first_word : first_word + P],
-                            ident[:],
-                        )
-                banks.append(flipped)
+            for g in range(PASSES):
+                for pair in range(BLOCKS // 2):
+                    flipped = flipped_pool.tile([P, 2, 2 * P], F32)
+                    for u in range(2):
+                        for n in range(2):
+                            first_word = (2 * g + u) * P
+                            nc.tensor.transpose(
+                                flipped[:, u, n * P : (n + 1) * P],
+                                rows[:, 2 * pair + n, :].bitcast(F32)[:, first_word : first_word + P],
+                                ident[:],
+                            )
+                    banks.append(flipped)
             return banks
 
-        def regroup(banks, grouped, g):
+        def empty(banks, grouped, g, pair):
             words = grouped[:, g, :].bitcast(F32).rearrange("p (c u) -> p c u", u=2)
-            for pair in range(BLOCKS // 2):
-                nc.scalar.copy(
-                    out=words[:, pair * 2 * P : (pair + 1) * 2 * P, :],
-                    in_=banks[pair][:].rearrange("p u c -> p c u"),
-                )
+            columns = words[:, pair * 2 * P : (pair + 1) * 2 * P, :]
+            bank = banks[2 * g + pair][:].rearrange("p u c -> p c u")
+            if (g, pair) == (PASSES - 1, BLOCKS // 2 - 1):
+                nc.scalar.copy(out=columns, in_=bank)
+            else:
+                nc.vector.tensor_copy(out=columns, in_=bank)
 
         def pack(grouped, codes, scales):
             nc.vector.quantize_mx(
@@ -83,25 +90,19 @@ def tile_prior_pb_t_kernel(
                 in_=grouped[:].rearrange("p g c -> p (g c)"),
             )
 
-        wh_rows = load_rows(W_h.rearrange("(p t) r -> p t r", t=H_TILES))
-        bh_bf16 = const.tile([P, H_TILES], BF16)
-        nc.scalar.dma_start(out=bh_bf16[:], in_=b_h.rearrange("(p t) -> p t", t=H_TILES))
         wo_rows = const.tile([P, H], BF16)
         nc.scalar.dma_start(out=wo_rows[:], in_=W_out)
-        bo = const.tile([P, 2 * S], BF16)
-        nc.scalar.dma_start(out=bo[:], in_=b_out.partition_broadcast(P))
-
-        wh_grouped = work.tile([P, PASSES, COLS * PACK], BF16, align_bytes=64, tag="grouped")
-        wh_codes = const.tile([P, PASSES, COLS], U32, align_bytes=64)
-        wh_scales = const.tile([P, PASSES, COLS], U8, align_bytes=64)
-        for g in range(PASSES):
-            regroup(flip(wh_rows, g), wh_grouped, g)
-        pack(wh_grouped, wh_codes, wh_scales)
-        bh = const.tile([P, H_TILES], F32)
-        nc.vector.tensor_copy(out=bh[:], in_=bh_bf16[:])
+        bh_bf16 = const.tile([P, H_TILES], BF16)
+        nc.scalar.dma_start(out=bh_bf16[:], in_=b_h.rearrange("(p t) -> p t", t=H_TILES))
+        bo_bf16 = const.tile([P, 2 * S], BF16)
+        nc.scalar.dma_start(out=bo_bf16[:], in_=b_out.partition_broadcast(P))
+        wh_rows = const.tile([P, H_TILES, R], BF16)
+        load_rows(wh_rows, W_h.rearrange("(p t) r -> p t r", t=H_TILES))
+        rows_of = {0: rows_pool.tile([P, BLOCKS, R], BF16, name="rows")}
+        load_rows(rows_of[0], x_rows[:, 0:BLOCKS, :])
 
         wo_words = wo_rows[:].bitcast(F32).rearrange("o (p u) -> o u p", u=2)
-        wo_flipped = flipped_pool.tile([P, 2, P], F32, tag="flipped")
+        wo_flipped = head_pool.tile([P, 2, P], F32, tag="head")
         for u in range(2):
             nc.tensor.transpose(wo_flipped[:, u, :], wo_words[:, u, :], ident[:])
         wo_grouped = const.tile([P, P * PACK], BF16, align_bytes=64)
@@ -109,68 +110,73 @@ def tile_prior_pb_t_kernel(
             out=wo_grouped[:].bitcast(F32).rearrange("p (o u) -> p o u", u=2),
             in_=wo_flipped[:].rearrange("p u o -> p o u"),
         )
+        bh = const.tile([P, H_TILES], F32)
+        nc.vector.tensor_copy(out=bh[:], in_=bh_bf16[:])
         wo_codes = const.tile([P, P], U32, align_bytes=64)
         wo_scales = const.tile([P, P], U8, align_bytes=64)
         nc.vector.quantize_mx(out=wo_codes[:].bitcast(FP8X4), scales=wo_scales[:], in_=wo_grouped[:])
 
-        rows_of, banks_of, grouped_of, packed_of = {}, {}, {}, {}
-        pre_of, grown_of, planes_of, h2_of, head_of, group_of = {}, {}, {}, {}, {}, {}
-        log1p_of = {}
+        wh_grouped = ahead.tile([P, PASSES, COLS * PACK], BF16, align_bytes=64, tag="grouped")
+        wh_codes = const.tile([P, PASSES, COLS], U32, align_bytes=64)
+        wh_scales = const.tile([P, PASSES, COLS], U8, align_bytes=64)
+        wh_banks = flip(wh_rows)
+        for g in range(PASSES):
+            for pair in range(BLOCKS // 2):
+                empty(wh_banks, wh_grouped, g, pair)
+        pack(wh_grouped, wh_codes, wh_scales)
 
-        def first_matmul(c):
+        bo = const.tile([P, 2 * S], F32)
+        nc.vector.tensor_copy(out=bo[:, 0:S], in_=bo_bf16[:, 0:S])
+        nc.vector.tensor_scalar_add(out=bo[:, S : 2 * S], in0=bo_bf16[:, S : 2 * S], scalar1=STD_MIN)
+
+        banks_of, grouped_of, packed_of, pre_of, halves_of = {}, {}, {}, {}, {}
+        joined_of, h2_of, head_of, group_of = {}, {}, {}, {}
+
+        def first_matmul(c, t):
             x_codes, x_scales = packed_of[c]
-            pre_of[c] = []
-            for t in range(H_TILES):
-                pre = pre_pool.tile([P, COLS], F32)
-                for g in range(PASSES):
-                    nc.tensor.matmul_mx(
-                        out=pre[:],
-                        lhsT=wh_codes[:, g, t * P : (t + 1) * P].bitcast(FP8X4),
-                        lhsT_scale=wh_scales[:, g, t * P : (t + 1) * P],
-                        rhs=x_codes[:, g, :].bitcast(FP8X4),
-                        rhs_scale=x_scales[:, g, :],
-                        start=(g == 0),
-                        stop=(g == PASSES - 1),
-                    )
-                pre_of[c].append(pre)
-
-        def grow(c):
-            grown = work.tile([P, H_TILES, COLS], F32)
-            for t in range(H_TILES):
-                nc.scalar.activation(
-                    out=grown[:, t, :], in_=pre_of[c][t][:], func=ACT.Exp, bias=bh[:, t : t + 1], scale=1.0
+            pre = pre_pool.tile([P, COLS], F32)
+            for g in range(PASSES):
+                nc.tensor.matmul_mx(
+                    out=pre[:],
+                    lhsT=wh_codes[:, g, t * P : (t + 1) * P].bitcast(FP8X4),
+                    lhsT_scale=wh_scales[:, g, t * P : (t + 1) * P],
+                    rhs=x_codes[:, g, :].bitcast(FP8X4),
+                    rhs_scale=x_scales[:, g, :],
+                    start=(g == 0),
+                    stop=(g == PASSES - 1),
                 )
-            grown_of[c] = grown
+            pre_of[c, t] = pre
 
-        def finish_elu(c):
-            below = work.tile([P, H_TILES, COLS], F32)
-            nc.vector.tensor_scalar(
-                out=below[:], in0=grown_of[c][:], scalar1=-1.0, scalar2=0.0, op0=ALU.add, op1=ALU.min
+        def elu_halves(c, t):
+            grown, kept = halves_of[c]
+            pre = pre_of[c, t]
+            nc.scalar.activation(
+                out=grown[:, t, :], in_=pre[:], func=ACT.Exp, bias=bh[:, t : t + 1], scale=1.0
             )
-            h2_planes = work.tile([P, H_TILES, COLS], BF16)
-            for t in range(H_TILES):
-                nc.vector.scalar_tensor_tensor(
-                    out=h2_planes[:, t, :],
-                    in0=pre_of[c][t][:],
-                    scalar=bh[:, t : t + 1],
-                    in1=below[:, t, :],
-                    op0=ALU.add,
-                    op1=ALU.max,
-                )
-            planes_of[c] = h2_planes
+            nc.scalar.activation(
+                out=kept[:, t, :], in_=pre[:], func=ACT.Relu, bias=bh[:, t : t + 1], scale=1.0
+            )
+
+        def join_elu(c):
+            grown, kept = halves_of[c]
+            h2 = work.tile([P, COLS, PACK], BF16, align_bytes=64)
+            nc.vector.scalar_tensor_tensor(
+                out=h2[:],
+                in0=grown[:].rearrange("p t c -> p c t"),
+                scalar=-1.0,
+                in1=kept[:].rearrange("p t c -> p c t"),
+                op0=ALU.add,
+                op1=ALU.min,
+            )
+            joined_of[c] = h2
 
         def pack_h2(c):
-            h2 = work.tile([P, COLS, PACK], BF16, align_bytes=64)
-            nc.vector.tensor_copy(
-                out=h2[:].rearrange("p (c i) t -> p c t i", i=4),
-                in_=planes_of[c][:].rearrange("p t (c i) -> p c t i", i=4),
-            )
             h2_codes = work.tile([P, COLS], U32, align_bytes=64)
             h2_scales = work.tile([P, COLS], U8, align_bytes=64)
             nc.vector.quantize_mx(
                 out=h2_codes[:].bitcast(FP8X4),
                 scales=h2_scales[:],
-                in_=h2[:].rearrange("p c t -> p (c t)"),
+                in_=joined_of[c][:].rearrange("p c t -> p (c t)"),
             )
             h2_of[c] = (h2_codes, h2_scales)
 
@@ -190,18 +196,28 @@ def tile_prior_pb_t_kernel(
             head_of[c] = head
 
         def open_group(group):
-            mean_pre = tail.tile([P, 2, GROUP_J, S], F32)
-            expneg = tail.tile([P, GROUP_J, S], F32)
-            floor = tail.tile([P, GROUP_J, S], F32)
-            noise = tail.tile([P, GROUP_J, S], BF16)
-            nc.sync.dma_start(out=noise[:], in_=eps_rows[:, group * GROUP_J : (group + 1) * GROUP_J, :])
-            group_of[group] = (mean_pre, expneg, floor, noise)
+            tiles = {
+                "o": tail.tile([P, 2, GROUP_J, S], F32, name="o"),
+                "capped": tail.tile([P, GROUP_J, S], F32, name="capped"),
+                "grown": tail.tile([P, GROUP_J, S], F32, name="grown_w"),
+                "log": tail.tile([P, GROUP_J, S], F32, name="log"),
+                "std": tail.tile([P, GROUP_J, S], F32, name="std"),
+                "sample": tail.tile([P, GROUP_J, S], F32, name="sample"),
+                "noise": tail.tile([P, GROUP_J, S], BF16, name="noise"),
+            }
+            nc.sync.dma_start(
+                out=tiles["noise"][:], in_=eps_rows[:, group * GROUP_J : (group + 1) * GROUP_J, :]
+            )
+            group_of[group] = tiles
+
+        def columns_of(c):
+            member = c % GROUP_CHUNKS
+            return group_of[c // GROUP_CHUNKS], slice(member * BLOCKS, (member + 1) * BLOCKS)
 
         def add_bias(c):
-            mean_pre, expneg, floor, noise = group_of[c // GROUP_CHUNKS]
-            js = slice((c % GROUP_CHUNKS) * BLOCKS, (c % GROUP_CHUNKS + 1) * BLOCKS)
+            tiles, js = columns_of(c)
             nc.vector.tensor_tensor(
-                out=mean_pre[:, :, js, :].rearrange("p half j s -> p j half s"),
+                out=tiles["o"][:, :, js, :].rearrange("p half j s -> p j half s"),
                 in0=head_of[c][:].rearrange("p j (half s) -> p j half s", half=2),
                 in1=bo[:]
                 .rearrange("p (half s) -> p half s", half=2)
@@ -210,37 +226,42 @@ def tile_prior_pb_t_kernel(
                 op=ALU.add,
             )
 
-        def soften(c):
-            mean_pre, expneg, floor, noise = group_of[c // GROUP_CHUNKS]
-            js = slice((c % GROUP_CHUNKS) * BLOCKS, (c % GROUP_CHUNKS + 1) * BLOCKS)
-            nc.scalar.activation(out=floor[:, js, :], in_=mean_pre[:, 1, js, :], func=ACT.Relu)
-            nc.scalar.activation(out=expneg[:, js, :], in_=mean_pre[:, 1, js, :], func=ACT.Abs)
-            nc.scalar.activation(out=expneg[:, js, :], in_=expneg[:, js, :], func=ACT.Exp, scale=-1.0)
+        def grow_w(c):
+            tiles, js = columns_of(c)
+            nc.vector.tensor_scalar_min(out=tiles["capped"][:, js, :], in0=tiles["o"][:, 1, js, :], scalar1=CAP)
+            nc.scalar.activation(out=tiles["grown"][:, js, :], in_=tiles["capped"][:, js, :], func=ACT.Exp)
 
         def take_logs(group):
-            mean_pre, expneg, floor, noise = group_of[group]
-            log1p = tail.tile([P, GROUP_J, S], F32)
-            nc.scalar.activation(out=log1p[:], in_=expneg[:], func=ACT.Ln, bias=1.0, scale=1.0)
-            log1p_of[group] = log1p
-
-        def finish_group(group):
-            mean_pre, expneg, floor, noise = group_of[group]
-            js = slice(group * GROUP_J, (group + 1) * GROUP_J)
-            nc.sync.dma_start(out=outs[0][:, js, :], in_=mean_pre[:, 0, :, :])
-            std = tail.tile([P, GROUP_J, S], F32)
-            nc.vector.scalar_tensor_tensor(
-                out=std[:].rearrange("p j s -> p (j s)"),
-                in0=floor[:].rearrange("p j s -> p (j s)"),
-                scalar=0.1,
-                in1=log1p_of[group][:].rearrange("p j s -> p (j s)"),
-                op0=ALU.add,
-                op1=ALU.add,
+            tiles = group_of[group]
+            nc.scalar.activation(
+                out=tiles["log"][:], in_=tiles["grown"][:], func=ACT.Ln, bias=1.0, scale=EXP_MINUS_STD_MIN
             )
-            nc.sync.dma_start(out=outs[1][:, js, :], in_=std[:])
-            sample = tail.tile([P, GROUP_J, S], F32)
-            nc.vector.tensor_tensor(out=sample[:], in0=std[:], in1=noise[:], op=ALU.mult)
-            nc.vector.tensor_tensor(out=sample[:], in0=sample[:], in1=mean_pre[:, 0, :, :], op=ALU.add)
-            nc.sync.dma_start(out=outs[2][:, js, :], in_=sample[:])
+
+        def finish_std(group):
+            tiles = group_of[group]
+            js = slice(group * GROUP_J, (group + 1) * GROUP_J)
+            nc.sync.dma_start(out=outs[0][:, js, :], in_=tiles["o"][:, 0, :, :])
+            nc.vector.scalar_tensor_tensor(
+                out=tiles["std"][:].rearrange("p j s -> p (j s)"),
+                in0=tiles["log"][:].rearrange("p j s -> p (j s)"),
+                scalar=STD_MIN,
+                in1=tiles["o"][:, 1, :, :].rearrange("p j s -> p (j s)"),
+                op0=ALU.add,
+                op1=ALU.max,
+            )
+            nc.sync.dma_start(out=outs[1][:, js, :], in_=tiles["std"][:])
+
+        def scale_noise(group):
+            tiles = group_of[group]
+            nc.vector.tensor_tensor(out=tiles["sample"][:], in0=tiles["std"][:], in1=tiles["noise"][:], op=ALU.mult)
+
+        def finish_sample(group):
+            tiles = group_of[group]
+            js = slice(group * GROUP_J, (group + 1) * GROUP_J)
+            nc.vector.tensor_tensor(
+                out=tiles["sample"][:], in0=tiles["sample"][:], in1=tiles["o"][:, 0, :, :], op=ALU.add
+            )
+            nc.sync.dma_start(out=outs[2][:, js, :], in_=tiles["sample"][:])
 
         def live(c):
             return 0 <= c < CHUNKS
@@ -248,38 +269,57 @@ def tile_prior_pb_t_kernel(
         def closes_group(c):
             return live(c) and c % GROUP_CHUNKS == GROUP_CHUNKS - 1
 
-        for i in range(-4, CHUNKS + 3):
+        def elu_and_next_matmul(i, banks):
+            for t in banks:
+                if live(i):
+                    elu_halves(i, t)
+                c_next, t_next = divmod(i * H_TILES + t + V_BANKS, H_TILES)
+                if live(c_next):
+                    first_matmul(c_next, t_next)
+
+        for i in range(-4, CHUNKS + 7):
+            if live(i + 5):
+                rows = rows_pool.tile([P, BLOCKS, R], BF16)
+                rows_of[i + 5] = rows
+                load_rows(rows, x_rows[:, (i + 5) * BLOCKS : (i + 6) * BLOCKS, :])
+            if live(i + 3):
+                grouped = ahead.tile([P, PASSES, COLS * PACK], BF16, align_bytes=64)
+                grouped_of[i + 3] = grouped
+                empty(banks_of[i + 3], grouped, 0, 0)
+                empty(banks_of[i + 3], grouped, 0, 1)
+            if live(i - 1):
+                join_elu(i - 1)
+            if live(i):
+                grown = work.tile([P, H_TILES, COLS], F32)
+                kept = work.tile([P, H_TILES, COLS], F32)
+                halves_of[i] = (grown, kept)
+            elu_and_next_matmul(i, (0, 1))
+            if live(i + 3):
+                empty(banks_of[i + 3], grouped_of[i + 3], 1, 0)
+                empty(banks_of[i + 3], grouped_of[i + 3], 1, 1)
+            if live(i - 1):
+                pack_h2(i - 1)
+            if live(i + 2):
+                x_codes = ahead.tile([P, PASSES, COLS], U32, align_bytes=64)
+                x_scales = ahead.tile([P, PASSES, COLS], U8, align_bytes=64)
+                packed_of[i + 2] = (x_codes, x_scales)
+                pack(grouped_of[i + 2], x_codes, x_scales)
             if live(i + 4):
-                rows_of[i + 4] = load_rows(x_rows[:, (i + 4) * BLOCKS : (i + 5) * BLOCKS, :])
+                banks_of[i + 4] = flip(rows_of[i + 4])
+            elu_and_next_matmul(i, (2, 3))
             if live(i - 2):
                 if (i - 2) % GROUP_CHUNKS == 0:
                     open_group((i - 2) // GROUP_CHUNKS)
                 add_bias(i - 2)
             if live(i - 1):
-                pack_h2(i - 1)
                 second_matmul(i - 1)
-            if live(i):
-                grow(i)
-            if live(i + 2):
-                grouped = work.tile([P, PASSES, COLS * PACK], BF16, align_bytes=64)
-                grouped_of[i + 2] = grouped
-                regroup(banks_of[i + 2], grouped, 0)
-                banks_of[i + 2] = flip(rows_of[i + 2], 1)
-            if live(i - 2):
-                soften(i - 2)
-            if closes_group(i - 2):
-                take_logs((i - 2) // GROUP_CHUNKS)
-            if live(i):
-                finish_elu(i)
-            if live(i + 1):
-                first_matmul(i + 1)
+            if live(i - 3):
+                grow_w(i - 3)
             if closes_group(i - 3):
-                finish_group((i - 3) // GROUP_CHUNKS)
-            if live(i + 2):
-                regroup(banks_of[i + 2], grouped_of[i + 2], 1)
-                x_codes = work.tile([P, PASSES, COLS], U32, align_bytes=64)
-                x_scales = work.tile([P, PASSES, COLS], U8, align_bytes=64)
-                packed_of[i + 2] = (x_codes, x_scales)
-                pack(grouped_of[i + 2], x_codes, x_scales)
-            if live(i + 3):
-                banks_of[i + 3] = flip(rows_of[i + 3], 0)
+                take_logs((i - 3) // GROUP_CHUNKS)
+            if closes_group(i - 4):
+                finish_std((i - 4) // GROUP_CHUNKS)
+            if closes_group(i - 5):
+                scale_noise((i - 5) // GROUP_CHUNKS)
+            if closes_group(i - 6):
+                finish_sample((i - 6) // GROUP_CHUNKS)

@@ -226,9 +226,12 @@ def tile_prior_pb_t_kernel(
                 op=ALU.add,
             )
 
-        def grow_w(c):
+        def cap_w(c):
             tiles, js = columns_of(c)
             nc.vector.tensor_scalar_min(out=tiles["capped"][:, js, :], in0=tiles["o"][:, 1, js, :], scalar1=CAP)
+
+        def grow_w(c):
+            tiles, js = columns_of(c)
             nc.scalar.activation(out=tiles["grown"][:, js, :], in_=tiles["capped"][:, js, :], func=ACT.Exp)
 
         def take_logs(group):
@@ -237,7 +240,7 @@ def tile_prior_pb_t_kernel(
                 out=tiles["log"][:], in_=tiles["grown"][:], func=ACT.Ln, bias=1.0, scale=EXP_MINUS_STD_MIN
             )
 
-        def finish_std(group):
+        def finish_group(group):
             tiles = group_of[group]
             js = slice(group * GROUP_J, (group + 1) * GROUP_J)
             nc.sync.dma_start(out=outs[0][:, js, :], in_=tiles["o"][:, 0, :, :])
@@ -250,14 +253,7 @@ def tile_prior_pb_t_kernel(
                 op1=ALU.max,
             )
             nc.sync.dma_start(out=outs[1][:, js, :], in_=tiles["std"][:])
-
-        def scale_noise(group):
-            tiles = group_of[group]
             nc.vector.tensor_tensor(out=tiles["sample"][:], in0=tiles["std"][:], in1=tiles["noise"][:], op=ALU.mult)
-
-        def finish_sample(group):
-            tiles = group_of[group]
-            js = slice(group * GROUP_J, (group + 1) * GROUP_J)
             nc.vector.tensor_tensor(
                 out=tiles["sample"][:], in0=tiles["sample"][:], in1=tiles["o"][:, 0, :, :], op=ALU.add
             )
@@ -277,11 +273,16 @@ def tile_prior_pb_t_kernel(
                 if live(c_next):
                     first_matmul(c_next, t_next)
 
-        for i in range(-4, CHUNKS + 7):
+        for i in range(-4, CHUNKS + 6):
             if live(i + 5):
                 rows = rows_pool.tile([P, BLOCKS, R], BF16)
                 rows_of[i + 5] = rows
                 load_rows(rows, x_rows[:, (i + 5) * BLOCKS : (i + 6) * BLOCKS, :])
+            if live(i + 2):
+                x_codes = ahead.tile([P, PASSES, COLS], U32, align_bytes=64)
+                x_scales = ahead.tile([P, PASSES, COLS], U8, align_bytes=64)
+                packed_of[i + 2] = (x_codes, x_scales)
+                pack(grouped_of[i + 2], x_codes, x_scales)
             if live(i + 3):
                 grouped = ahead.tile([P, PASSES, COLS * PACK], BF16, align_bytes=64)
                 grouped_of[i + 3] = grouped
@@ -299,11 +300,6 @@ def tile_prior_pb_t_kernel(
                 empty(banks_of[i + 3], grouped_of[i + 3], 1, 1)
             if live(i - 1):
                 pack_h2(i - 1)
-            if live(i + 2):
-                x_codes = ahead.tile([P, PASSES, COLS], U32, align_bytes=64)
-                x_scales = ahead.tile([P, PASSES, COLS], U8, align_bytes=64)
-                packed_of[i + 2] = (x_codes, x_scales)
-                pack(grouped_of[i + 2], x_codes, x_scales)
             if live(i + 4):
                 banks_of[i + 4] = flip(rows_of[i + 4])
             elu_and_next_matmul(i, (2, 3))
@@ -314,12 +310,10 @@ def tile_prior_pb_t_kernel(
             if live(i - 1):
                 second_matmul(i - 1)
             if live(i - 3):
-                grow_w(i - 3)
-            if closes_group(i - 3):
-                take_logs((i - 3) // GROUP_CHUNKS)
+                cap_w(i - 3)
+            if live(i - 4):
+                grow_w(i - 4)
             if closes_group(i - 4):
-                finish_std((i - 4) // GROUP_CHUNKS)
+                take_logs((i - 4) // GROUP_CHUNKS)
             if closes_group(i - 5):
-                scale_noise((i - 5) // GROUP_CHUNKS)
-            if closes_group(i - 6):
-                finish_sample((i - 6) // GROUP_CHUNKS)
+                finish_group((i - 5) // GROUP_CHUNKS)

@@ -78,7 +78,7 @@ def tile_prior_pb_t_kernel(
             words = grouped[:, g, :].bitcast(F32).rearrange("p (c u) -> p c u", u=2)
             columns = words[:, pair * 2 * P : (pair + 1) * 2 * P, :]
             bank = banks[2 * g + pair][:].rearrange("p u c -> p c u")
-            if (g, pair) == (PASSES - 1, BLOCKS // 2 - 1):
+            if pair == 1:
                 nc.scalar.copy(out=columns, in_=bank)
             else:
                 nc.vector.tensor_copy(out=columns, in_=bank)
@@ -273,7 +273,7 @@ def tile_prior_pb_t_kernel(
                 if live(c_next):
                     first_matmul(c_next, t_next)
 
-        for i in range(-4, CHUNKS + 6):
+        for i in range(-4, CHUNKS + 5):
             if live(i + 5):
                 rows = rows_pool.tile([P, BLOCKS, R], BF16)
                 rows_of[i + 5] = rows

@@ -45,7 +45,7 @@ def tile_prior_pb_t_kernel(
         rows_pool = ctx.enter_context(tc.tile_pool(name="rows", bufs=4))
         ahead = ctx.enter_context(tc.tile_pool(name="ahead", bufs=3))
         work = ctx.enter_context(tc.tile_pool(name="work", bufs=2))
-        tail = ctx.enter_context(tc.tile_pool(name="tail", bufs=2))
+        tail = ctx.enter_context(tc.tile_pool(name="tail", bufs=3))
         flipped_pool = ctx.enter_context(tc.psum_pool(name="flipped", bufs=PASSES * BLOCKS // 2))
         pre_pool = ctx.enter_context(tc.psum_pool(name="pre", bufs=V_BANKS))
         head_pool = ctx.enter_context(tc.psum_pool(name="head", bufs=1))
@@ -273,7 +273,7 @@ def tile_prior_pb_t_kernel(
                 if live(c_next):
                     first_matmul(c_next, t_next)
 
-        for i in range(-4, CHUNKS + 5):
+        for i in range(-4, CHUNKS + 7):
             if live(i + 5):
                 rows = rows_pool.tile([P, BLOCKS, R], BF16)
                 rows_of[i + 5] = rows
@@ -315,5 +315,5 @@ def tile_prior_pb_t_kernel(
                 grow_w(i - 4)
             if closes_group(i - 4):
                 take_logs((i - 4) // GROUP_CHUNKS)
-            if closes_group(i - 5):
-                finish_group((i - 5) // GROUP_CHUNKS)
+            if closes_group(i - 7):
+                finish_group((i - 7) // GROUP_CHUNKS)

@@ -130,7 +130,7 @@ def tile_prior_pb_t_kernel(
         nc.vector.tensor_scalar_add(out=bo[:, S : 2 * S], in0=bo_bf16[:, S : 2 * S], scalar1=STD_MIN)
 
         banks_of, grouped_of, packed_of, pre_of, halves_of = {}, {}, {}, {}, {}
-        joined_of, h2_of, head_of, group_of = {}, {}, {}, {}
+        planes_of, joined_of, h2_of, head_of, group_of = {}, {}, {}, {}, {}
 
         def first_matmul(c, t):
             x_codes, x_scales = packed_of[c]
@@ -159,14 +159,22 @@ def tile_prior_pb_t_kernel(
 
         def join_elu(c):
             grown, kept = halves_of[c]
-            h2 = work.tile([P, COLS, PACK], BF16, align_bytes=64)
+            h2_planes = work.tile([P, H_TILES, COLS], BF16)
             nc.vector.scalar_tensor_tensor(
-                out=h2[:],
-                in0=grown[:].rearrange("p t c -> p c t"),
+                out=h2_planes[:].rearrange("p t c -> p (t c)"),
+                in0=grown[:].rearrange("p t c -> p (t c)"),
                 scalar=-1.0,
-                in1=kept[:].rearrange("p t c -> p c t"),
+                in1=kept[:].rearrange("p t c -> p (t c)"),
                 op0=ALU.add,
                 op1=ALU.min,
+            )
+            planes_of[c] = h2_planes
+
+        def regroup_h2(c):
+            h2 = work.tile([P, COLS, PACK], BF16, align_bytes=64)
+            nc.vector.tensor_copy(
+                out=h2[:].rearrange("p (c i) t -> p c t i", i=4),
+                in_=planes_of[c][:].rearrange("p t (c i) -> p c t i", i=4),
             )
             joined_of[c] = h2
 
@@ -299,14 +307,16 @@ def tile_prior_pb_t_kernel(
                 empty(banks_of[i + 3], grouped_of[i + 3], 1, 0)
                 empty(banks_of[i + 3], grouped_of[i + 3], 1, 1)
             if live(i - 1):
-                pack_h2(i - 1)
-            if live(i + 4):
-                banks_of[i + 4] = flip(rows_of[i + 4])
-            elu_and_next_matmul(i, (2, 3))
+                regroup_h2(i - 1)
             if live(i - 2):
                 if (i - 2) % GROUP_CHUNKS == 0:
                     open_group((i - 2) // GROUP_CHUNKS)
                 add_bias(i - 2)
+            if live(i - 1):
+                pack_h2(i - 1)
+            if live(i + 4):
+                banks_of[i + 4] = flip(rows_of[i + 4])
+            elu_and_next_matmul(i, (2, 3))
             if live(i - 1):
                 second_matmul(i - 1)
             if live(i - 3):

from contextlib import ExitStack

import concourse.mybir as mybir
from concourse.masks import make_identity

F32 = mybir.dt.float32
BF16 = mybir.dt.bfloat16
U32 = mybir.dt.uint32
U8 = mybir.dt.uint8
FP8X4 = mybir.dt.float8_e4m3fn_x4
ACT = mybir.ActivationFunctionType
ALU = mybir.AluOpType

BATCH, R, H, S = 8192, 1024, 512, 64
P = 128
PACK = 4
K_PASS = P * PACK
PASSES = R // K_PASS
BLOCKS = 4
COLS = BLOCKS * P
H_TILES = H // P
J = BATCH // P
CHUNKS = J // BLOCKS
GROUP_CHUNKS = 4
GROUP_J = GROUP_CHUNKS * BLOCKS
V_BANKS = 3
STD_MIN = 0.1
EXP_MINUS_STD_MIN = 0.9048374180359595
CAP = 30.0

FLOPS = 2 * BATCH * R * H + 2 * BATCH * H * 2 * S


def tile_prior_pb_t_kernel(
    tc, rnn_hidden, eps, W_h, b_h, W_out, b_out, out_0, out_1, out_2
):
    nc = tc.nc
    x_rows = rnn_hidden.rearrange("(p j) r -> p j r", j=J)
    eps_rows = eps.rearrange("(p j) s -> p j s", j=J)
    outs = [o.rearrange("(p j) s -> p j s", j=J) for o in (out_0, out_1, out_2)]

    with ExitStack() as ctx:
        ctx.enter_context(tc.manual_schedule())
        const = ctx.enter_context(tc.tile_pool(name="const", bufs=1))
        rows_pool = ctx.enter_context(tc.tile_pool(name="rows", bufs=4))
        ahead = ctx.enter_context(tc.tile_pool(name="ahead", bufs=3))
        work = ctx.enter_context(tc.tile_pool(name="work", bufs=2))
        tail = ctx.enter_context(tc.tile_pool(name="tail", bufs=3))
        flipped_pool = ctx.enter_context(tc.psum_pool(name="flipped", bufs=PASSES * BLOCKS // 2))
        pre_pool = ctx.enter_context(tc.psum_pool(name="pre", bufs=V_BANKS))
        head_pool = ctx.enter_context(tc.psum_pool(name="head", bufs=1))

        ident = const.tile([P, P], F32)
        make_identity(nc, ident[:])

        def load_rows(rows, dram_rows):
            for g in range(PASSES):
                ks = slice(g * K_PASS, (g + 1) * K_PASS)
                nc.sync.dma_start(out=rows[:, :, ks], in_=dram_rows[:, :, ks])

        def flip(rows):
            banks = []
            for g in range(PASSES):
                for pair in range(BLOCKS // 2):
                    flipped = flipped_pool.tile([P, 2, 2 * P], F32)
                    for u in range(2):
                        for n in range(2):
                            first_word = (2 * g + u) * P
                            nc.tensor.transpose(
                                flipped[:, u, n * P : (n + 1) * P],
                                rows[:, 2 * pair + n, :].bitcast(F32)[:, first_word : first_word + P],
                                ident[:],
                            )
                    banks.append(flipped)
            return banks

        def empty(banks, grouped, g, pair):
            words = grouped[:, g, :].bitcast(F32).rearrange("p (c u) -> p c u", u=2)
            columns = words[:, pair * 2 * P : (pair + 1) * 2 * P, :]
            bank = banks[2 * g + pair][:].rearrange("p u c -> p c u")
            if pair == 1:
                nc.scalar.copy(out=columns, in_=bank)
            else:
                nc.vector.tensor_copy(out=columns, in_=bank)

        def pack(grouped, codes, scales):
            nc.vector.quantize_mx(
                out=codes[:].rearrange("p g c -> p (g c)").bitcast(FP8X4),
                scales=scales[:].rearrange("p g c -> p (g c)"),
                in_=grouped[:].rearrange("p g c -> p (g c)"),
            )

        wo_rows = const.tile([P, H], BF16)
        nc.scalar.dma_start(out=wo_rows[:], in_=W_out)
        bh_bf16 = const.tile([P, H_TILES], BF16)
        nc.scalar.dma_start(out=bh_bf16[:], in_=b_h.rearrange("(p t) -> p t", t=H_TILES))
        bo_bf16 = const.tile([P, 2 * S], BF16)
        nc.scalar.dma_start(out=bo_bf16[:], in_=b_out.partition_broadcast(P))
        wh_rows = const.tile([P, H_TILES, R], BF16)
        load_rows(wh_rows, W_h.rearrange("(p t) r -> p t r", t=H_TILES))
        rows_of = {0: rows_pool.tile([P, BLOCKS, R], BF16, name="rows")}
        load_rows(rows_of[0], x_rows[:, 0:BLOCKS, :])

        wo_words = wo_rows[:].bitcast(F32).rearrange("o (p u) -> o u p", u=2)
        wo_flipped = head_pool.tile([P, 2, P], F32, tag="head")
        for u in range(2):
            nc.tensor.transpose(wo_flipped[:, u, :], wo_words[:, u, :], ident[:])
        wo_grouped = const.tile([P, P * PACK], BF16, align_bytes=64)
        nc.vector.tensor_copy(
            out=wo_grouped[:].bitcast(F32).rearrange("p (o u) -> p o u", u=2),
            in_=wo_flipped[:].rearrange("p u o -> p o u"),
        )
        bh = const.tile([P, H_TILES], F32)
        nc.vector.tensor_copy(out=bh[:], in_=bh_bf16[:])
        wo_codes = const.tile([P, P], U32, align_bytes=64)
        wo_scales = const.tile([P, P], U8, align_bytes=64)
        nc.vector.quantize_mx(out=wo_codes[:].bitcast(FP8X4), scales=wo_scales[:], in_=wo_grouped[:])

        wh_grouped = ahead.tile([P, PASSES, COLS * PACK], BF16, align_bytes=64, tag="grouped")
        wh_codes = const.tile([P, PASSES, COLS], U32, align_bytes=64)
        wh_scales = const.tile([P, PASSES, COLS], U8, align_bytes=64)
        wh_banks = flip(wh_rows)
        for g in range(PASSES):
            for pair in range(BLOCKS // 2):
                empty(wh_banks, wh_grouped, g, pair)
        pack(wh_grouped, wh_codes, wh_scales)

        bo = const.tile([P, 2 * S], F32)
        nc.vector.tensor_copy(out=bo[:, 0:S], in_=bo_bf16[:, 0:S])
        nc.vector.tensor_scalar_add(out=bo[:, S : 2 * S], in0=bo_bf16[:, S : 2 * S], scalar1=STD_MIN)

        banks_of, grouped_of, packed_of, pre_of, halves_of = {}, {}, {}, {}, {}
        planes_of, joined_of, h2_of, head_of, group_of = {}, {}, {}, {}, {}

        def first_matmul(c, t):
            x_codes, x_scales = packed_of[c]
            pre = pre_pool.tile([P, COLS], F32)
            for g in range(PASSES):
                nc.tensor.matmul_mx(
                    out=pre[:],
                    lhsT=wh_codes[:, g, t * P : (t + 1) * P].bitcast(FP8X4),
                    lhsT_scale=wh_scales[:, g, t * P : (t + 1) * P],
                    rhs=x_codes[:, g, :].bitcast(FP8X4),
                    rhs_scale=x_scales[:, g, :],
                    start=(g == 0),
                    stop=(g == PASSES - 1),
                )
            pre_of[c, t] = pre

        def elu_halves(c, t):
            grown, kept = halves_of[c]
            pre = pre_of[c, t]
            nc.scalar.activation(
                out=grown[:, t, :], in_=pre[:], func=ACT.Exp, bias=bh[:, t : t + 1], scale=1.0
            )
            nc.scalar.activation(
                out=kept[:, t, :], in_=pre[:], func=ACT.Relu, bias=bh[:, t : t + 1], scale=1.0
            )

        def join_elu(c):
            grown, kept = halves_of[c]
            h2_planes = work.tile([P, H_TILES, COLS], BF16)
            nc.vector.scalar_tensor_tensor(
                out=h2_planes[:].rearrange("p t c -> p (t c)"),
                in0=grown[:].rearrange("p t c -> p (t c)"),
                scalar=-1.0,
                in1=kept[:].rearrange("p t c -> p (t c)"),
                op0=ALU.add,
                op1=ALU.min,
            )
            planes_of[c] = h2_planes

        def regroup_h2(c):
            h2 = work.tile([P, COLS, PACK], BF16, align_bytes=64)
            nc.vector.tensor_copy(
                out=h2[:].rearrange("p (c i) t -> p c t i", i=4),
                in_=planes_of[c][:].rearrange("p t (c i) -> p c t i", i=4),
            )
            joined_of[c] = h2

        def pack_h2(c):
            h2_codes = work.tile([P, COLS], U32, align_bytes=64)
            h2_scales = work.tile([P, COLS], U8, align_bytes=64)
            nc.vector.quantize_mx(
                out=h2_codes[:].bitcast(FP8X4),
                scales=h2_scales[:],
                in_=joined_of[c][:].rearrange("p c t -> p (c t)"),
            )
            h2_of[c] = (h2_codes, h2_scales)

        def second_matmul(c):
            h2_codes, h2_scales = h2_of[c]
            head = head_pool.tile([P, BLOCKS, 2 * S], F32)
            for n in range(BLOCKS):
                nc.tensor.matmul_mx(
                    out=head[:, n, :],
                    lhsT=h2_codes[:, n * P : (n + 1) * P].bitcast(FP8X4),
                    lhsT_scale=h2_scales[:, n * P : (n + 1) * P],
                    rhs=wo_codes[:].bitcast(FP8X4),
                    rhs_scale=wo_scales[:],
                    start=True,
                    stop=True,
                )
            head_of[c] = head

        def open_group(group):
            tiles = {
                "o": tail.tile([P, 2, GROUP_J, S], F32, name="o"),
                "capped": tail.tile([P, GROUP_J, S], F32, name="capped"),
                "grown": tail.tile([P, GROUP_J, S], F32, name="grown_w"),
                "log": tail.tile([P, GROUP_J, S], F32, name="log"),
                "std": tail.tile([P, GROUP_J, S], F32, name="std"),
                "sample": tail.tile([P, GROUP_J, S], F32, name="sample"),
                "noise": tail.tile([P, GROUP_J, S], BF16, name="noise"),
            }
            nc.sync.dma_start(
                out=tiles["noise"][:], in_=eps_rows[:, group * GROUP_J : (group + 1) * GROUP_J, :]
            )
            group_of[group] = tiles

        def columns_of(c):
            member = c % GROUP_CHUNKS
            return group_of[c // GROUP_CHUNKS], slice(member * BLOCKS, (member + 1) * BLOCKS)

        def add_bias(c):
            tiles, js = columns_of(c)
            nc.vector.tensor_tensor(
                out=tiles["o"][:, :, js, :].rearrange("p half j s -> p j half s"),
                in0=head_of[c][:].rearrange("p j (half s) -> p j half s", half=2),
                in1=bo[:]
                .rearrange("p (half s) -> p half s", half=2)
                .unsqueeze(1)
                .to_broadcast([P, BLOCKS, 2, S]),
                op=ALU.add,
            )

        def cap_w(c):
            tiles, js = columns_of(c)
            nc.vector.tensor_scalar_min(out=tiles["capped"][:, js, :], in0=tiles["o"][:, 1, js, :], scalar1=CAP)

        def grow_w(c):
            tiles, js = columns_of(c)
            nc.scalar.activation(out=tiles["grown"][:, js, :], in_=tiles["capped"][:, js, :], func=ACT.Exp)

        def take_logs(group):
            tiles = group_of[group]
            nc.scalar.activation(
                out=tiles["log"][:], in_=tiles["grown"][:], func=ACT.Ln, bias=1.0, scale=EXP_MINUS_STD_MIN
            )

        def finish_group(group):
            tiles = group_of[group]
            js = slice(group * GROUP_J, (group + 1) * GROUP_J)
            nc.sync.dma_start(out=outs[0][:, js, :], in_=tiles["o"][:, 0, :, :])
            nc.vector.scalar_tensor_tensor(
                out=tiles["std"][:].rearrange("p j s -> p (j s)"),
                in0=tiles["log"][:].rearrange("p j s -> p (j s)"),
                scalar=STD_MIN,
                in1=tiles["o"][:, 1, :, :].rearrange("p j s -> p (j s)"),
                op0=ALU.add,
                op1=ALU.max,
            )
            nc.sync.dma_start(out=outs[1][:, js, :], in_=tiles["std"][:])
            nc.vector.tensor_tensor(out=tiles["sample"][:], in0=tiles["std"][:], in1=tiles["noise"][:], op=ALU.mult)
            nc.vector.tensor_tensor(
                out=tiles["sample"][:], in0=tiles["sample"][:], in1=tiles["o"][:, 0, :, :], op=ALU.add
            )
            nc.sync.dma_start(out=outs[2][:, js, :], in_=tiles["sample"][:])

        def live(c):
            return 0 <= c < CHUNKS

        def closes_group(c):
            return live(c) and c % GROUP_CHUNKS == GROUP_CHUNKS - 1

        def elu_and_next_matmul(i, banks):
            for t in banks:
                if live(i):
                    elu_halves(i, t)
                c_next, t_next = divmod(i * H_TILES + t + V_BANKS, H_TILES)
                if live(c_next):
                    first_matmul(c_next, t_next)

        for i in range(-4, CHUNKS + 7):
            if live(i + 5):
                rows = rows_pool.tile([P, BLOCKS, R], BF16)
                rows_of[i + 5] = rows
                load_rows(rows, x_rows[:, (i + 5) * BLOCKS : (i + 6) * BLOCKS, :])
            if live(i + 2):
                x_codes = ahead.tile([P, PASSES, COLS], U32, align_bytes=64)
                x_scales = ahead.tile([P, PASSES, COLS], U8, align_bytes=64)
                packed_of[i + 2] = (x_codes, x_scales)
                pack(grouped_of[i + 2], x_codes, x_scales)
            if live(i + 3):
                grouped = ahead.tile([P, PASSES, COLS * PACK], BF16, align_bytes=64)
                grouped_of[i + 3] = grouped
                empty(banks_of[i + 3], grouped, 0, 0)
                empty(banks_of[i + 3], grouped, 0, 1)
            if live(i - 1):
                join_elu(i - 1)
            if live(i):
                grown = work.tile([P, H_TILES, COLS], F32)
                kept = work.tile([P, H_TILES, COLS], F32)
                halves_of[i] = (grown, kept)
            elu_and_next_matmul(i, (0, 1))
            if live(i + 3):
                empty(banks_of[i + 3], grouped_of[i + 3], 1, 0)
                empty(banks_of[i + 3], grouped_of[i + 3], 1, 1)
            if live(i - 1):
                regroup_h2(i - 1)
            if live(i - 2):
                if (i - 2) % GROUP_CHUNKS == 0:
                    open_group((i - 2) // GROUP_CHUNKS)
                add_bias(i - 2)
            if live(i - 1):
                pack_h2(i - 1)
            if live(i + 4):
                banks_of[i + 4] = flip(rows_of[i + 4])
            elu_and_next_matmul(i, (2, 3))
            if live(i - 1):
                second_matmul(i - 1)
            if live(i - 3):
                cap_w(i - 3)
            if live(i - 4):
                grow_w(i - 4)
            if closes_group(i - 4):
                take_logs((i - 4) // GROUP_CHUNKS)
            if closes_group(i - 7):
                finish_group((i - 7) // GROUP_CHUNKS)
